import numpy as np
import ml_dtypes


def mxq(x, axis, fmt="e4m3"):
    dtype, down = {"e4m3": (ml_dtypes.float8_e4m3fn, 7), "e5m2": (ml_dtypes.float8_e5m2, 14)}[fmt]
    v = np.moveaxis(np.asarray(x, np.float32).astype(ml_dtypes.bfloat16).astype(np.float64), axis, -1)
    blocks = v.reshape(v.shape[:-1] + (-1, 32))
    amax = np.abs(blocks).max(-1, keepdims=True)
    byte = np.maximum(np.where(amax > 0, np.frexp(amax)[1] - 1 + 127, 0) - down, 1)
    scale = np.exp2(byte - 127.0)
    codes = (blocks / scale).astype(np.float32).astype(dtype).astype(np.float64)
    return np.moveaxis((codes * scale).reshape(v.shape), -1, axis)


WIDE = False


def mx_kscale(k):
    if not WIDE:
        return np.ones(k)
    levels = np.array([10, -10, 5, -5, 0])
    if k % 512:
        return np.exp2(np.random.permutation(np.resize(levels, k // 32))).repeat(32)
    a = np.empty((k // 512, 16))
    for p in range(k // 512):
        a[p, :8] = np.random.permutation(np.resize(levels, 8))
        for g in range(8):
            far = levels[np.abs(levels - a[p, g]) >= 10]
            a[p, g + 8] = far[np.random.randint(len(far))]
    return np.exp2(a.ravel()).repeat(32)


BF16 = ml_dtypes.bfloat16


def bf(x):
    return np.asarray(x, np.float32).astype(BF16)


def f64(x):
    return np.asarray(x).astype(np.float64)


B, W, U, H, D, K, MAX_BACK, MAX_FWD = 2, 4, 128, 4, 512, 256, 127, 0
CH = H * D
F = MAX_BACK + MAX_FWD + 1


def setup_inputs():
    s, t = mx_kscale(CH), mx_kscale(D)
    a = 1.5 * D ** -0.25
    return {"queries": bf(np.random.standard_normal((B, W, U, H, D)) * a * t),
            "keys": bf(np.random.standard_normal((B, W, K, H, D)) * a / t),
            "sin_emb": bf(np.random.standard_normal((F, CH)) * np.sqrt(0.5) * s),
            "pos_w": bf(np.random.standard_normal((CH, CH)) * 2.0 * D ** -0.25 / np.sqrt(CH) / s[None, :] / np.tile(t, H)[:, None])}


def relative_shift(x):
    pad = K + 1 - F
    x = np.pad(x, ((0, 0), (0, 0), (0, 0), (0, 0), (0, pad)))
    x = x.reshape(B, H, W, U * (K + 1))[:, :, :, : U * K]
    return x.reshape(B, H, W, U, K)


def reference(queries, keys, sin_emb, pos_w):
    proj = (mxq(f64(sin_emb), 1, "e4m3") @ mxq(f64(pos_w), 1, "e4m3").T).reshape(F, H, D)
    qq = mxq(f64(queries), 4, "e4m3").transpose(0, 3, 1, 2, 4)
    kq = mxq(f64(keys), 4, "e4m3").transpose(0, 3, 1, 4, 2)
    pq = mxq(proj, 2, "e4m3").transpose(1, 2, 0)[None, :, None]
    term_ac = qq @ kq
    term_bd = qq @ pq
    return term_ac + relative_shift(term_bd)

@@ -1,0 +1,237 @@
+from contextlib import ExitStack
+
+import concourse.mybir as mybir
+from concourse.masks import make_identity
+
+F32 = mybir.dt.float32
+BF16 = mybir.dt.bfloat16
+U32 = mybir.dt.uint32
+U8 = mybir.dt.uint8
+FP8X4 = mybir.dt.float8_e4m3fn_x4
+
+P = 128
+B, W, U, H, D, KC, F = 2, 4, 128, 4, 512, 256, 128
+CH = H * D
+PITCH = 160
+WIN = PITCH - 1
+QUAD = 32
+GROUPS = U // QUAD
+PAIR_ROW = 2 * H * PITCH
+PAIR = U * PAIR_ROW
+SCRATCH = B * H * W * U * KC - 4 * PAIR - 4096
+
+N_W, N_Q, N_K = 8, 4, 8
+N_TILES = N_W + N_Q + N_K
+DEPTH = 4
+
+FLOPS = 2 * F * CH * CH + B * W * H * 2 * U * D * (KC + F)
+
+
+def tile_gemma3naudiorelativepositionembedding_pa_kernel(tc, queries, keys, sin_emb, pos_w, out):
+    nc = tc.nc
+    with ExitStack() as ctx:
+        const = ctx.enter_context(tc.tile_pool(name="const", bufs=1))
+        rawp = ctx.enter_context(tc.tile_pool(name="rawp", bufs=DEPTH))
+        grp = ctx.enter_context(tc.tile_pool(name="grp", bufs=3))
+        cod = ctx.enter_context(tc.tile_pool(name="cod", bufs=3))
+        outp = ctx.enter_context(tc.tile_pool(name="outp", bufs=3))
+        psum_t = ctx.enter_context(tc.psum_pool(name="psumt", bufs=4))
+        psum_a = ctx.enter_context(tc.psum_pool(name="psuma", bufs=4))
+        ctx.enter_context(tc.manual_schedule())
+
+        outflat = out.rearrange("b h w u c -> (b h w u c)")
+        raw, grouped, codes, scales, banks = {}, {}, {}, {}, {}
+
+        def load(t):
+            raw[t] = rawp.tile([P, 2, CH], BF16, name="raw", tag="raw")
+            if t < N_W:
+                four = pos_w[D * (t // 2) : D * (t // 2 + 1), :].rearrange("(p e) c -> p e c", e=4)
+                src = four[:, 2 * (t % 2) : 2 * (t % 2) + 2, :]
+            elif t < N_W + N_Q:
+                j = t - N_W
+                src = queries[j // 2, 2 * (j % 2) : 2 * (j % 2) + 2].rearrange("s u h d -> u s (h d)")
+            else:
+                bw = t - N_W - N_Q
+                src = keys[bw // W, bw % W].rearrange("(p e) h d -> p e (h d)", e=2)
+            nc.sync.dma_start(out=raw[t][:], in_=src)
+
+        sraw = const.tile([P, CH], BF16)
+        nc.sync.dma_start(out=sraw[:], in_=sin_emb)
+        for t in range(DEPTH):
+            load(t)
+
+        ident = const.tile([P, P], F32)
+        make_identity(nc, ident[:])
+        perm = const.tile([P, P], F32)
+        nc.vector.tensor_copy(
+            out=perm[:].rearrange("p (r a) -> p a r", a=GROUPS), in_=ident[:].rearrange("p (a r) -> p a r", a=GROUPS)
+        )
+        shifted = const.tile([P, B * W * H, KC], F32)
+        stages = []
+        for n in range(2):
+            stage = const.tile([P, 2 * H, PITCH], F32, name="stage%d" % n)
+            nc.vector.memset(stage[:, :, F:PITCH], 0.0)
+            stages.append(stage)
+
+        qcodes = const.tile([P, N_Q, 2 * H * U], U32, align_bytes=64)
+        qscales = const.tile([P, N_Q, 2 * H * U], U8, align_bytes=64)
+        scodes = const.tile([P, 4 * F], U32, align_bytes=64)
+        sscales = const.tile([P, 4 * F], U8, align_bytes=64)
+        pcodes = const.tile([P, H * F], U32, align_bytes=64)
+        pscales = const.tile([P, H * F], U8, align_bytes=64)
+
+        def copy_out(on_vector, dst, src):
+            if on_vector:
+                nc.vector.tensor_copy(out=dst, in_=src)
+            else:
+                nc.scalar.copy(out=dst, in_=src)
+
+        def transpose_rows(words, first, eye, dst, on_vector):
+            bank = psum_t.tile([P, 2, 2, P], F32, name="xt", tag="xt")
+            for x in range(2):
+                for u in range(2):
+                    w0 = (first + 2 * x) * P
+                    nc.tensor.transpose(bank[:, x, u, :], words[:, w0 + u : w0 + 2 * P : 2], eye[:])
+            copy_out(on_vector, dst, bank[:].rearrange("p x u r -> p x r u"))
+
+        def transpose_keys(t, h, dst, on_vector):
+            bank = psum_t.tile([P, 2, 2, P], F32, name="xt", tag="xt")
+            for e in range(2):
+                for u in range(2):
+                    w0 = 2 * h * P
+                    nc.tensor.transpose(
+                        bank[:, e, u, :], raw[t][:, e, :].bitcast(F32)[:, w0 + u : w0 + 2 * P : 2], ident[:]
+                    )
+            copy_out(on_vector, dst, bank[:].rearrange("p e u r -> p r e u"))
+
+        def transpose(t):
+            grouped[t] = grp.tile([P, 4, 2 * P, 4], BF16, name="grouped", tag="grouped", align_bytes=64)
+            words = grouped[t][:].bitcast(F32)
+            for n in range(4):
+                if t < N_W + N_Q:
+                    dst = words[:, n, :, :].rearrange("p (x r) u -> p x r u", x=2)
+                    eye = ident if t < N_W else perm
+                    on_vector = t >= N_W and n >= 2
+                    transpose_rows(raw[t][:, n // 2, :].bitcast(F32), 4 * (n % 2), eye, dst, on_vector)
+                else:
+                    dst = words[:, n, :, :].rearrange("p (r e) u -> p r e u", e=2)
+                    transpose_keys(t, n, dst, False)
+
+        def quantise(t):
+            if N_W <= t < N_W + N_Q:
+                codes[t], scales[t] = qcodes[:, t - N_W, :], qscales[:, t - N_W, :]
+            else:
+                ctile = cod.tile([P, 8 * P], U32, name="ctile", tag="ctile", align_bytes=64)
+                stile = cod.tile([P, 8 * P], U8, name="stile", tag="stile", align_bytes=64)
+                codes[t], scales[t] = ctile[:], stile[:]
+            for n in range(2):
+                cols = slice(4 * P * n, 4 * P * (n + 1))
+                nc.vector.quantize_mx(
+                    out=codes[t][:, cols].bitcast(FP8X4),
+                    scales=scales[t][:, cols],
+                    in_=grouped[t][:, 2 * n : 2 * n + 2].rearrange("p n c t -> p (n c t)"),
+                )
+
+        def mx(dst, t_l, l0, t_r, r0, n, start, stop):
+            nc.tensor.matmul_mx(
+                out=dst,
+                lhsT=codes[t_l][:, l0 : l0 + P].bitcast(FP8X4),
+                lhsT_scale=scales[t_l][:, l0 : l0 + P],
+                rhs=codes[t_r][:, r0 : r0 + n].bitcast(FP8X4),
+                rhs_scale=scales[t_r][:, r0 : r0 + n],
+                start=start,
+                stop=stop,
+            )
+
+        def multiply(t):
+            if t < N_W:
+                if t % 2 == 0:
+                    banks[t + 1] = psum_a.tile([P, 4, F], F32, name="acc", tag="acc")
+                for e in range(2):
+                    for c in range(4):
+                        mx(banks[t | 1][:, 2 * (t % 2) + e, :], t, (4 * e + c) * P, "sin", c * P, F, c == 0, c == 3)
+            elif t < N_W + N_Q:
+                for s in range(2):
+                    banks[(t, s)] = psum_a.tile([P, H, F], F32, name="acc", tag="acc")
+                    for h in range(H):
+                        mx(banks[(t, s)][:, h, :], t, (H * s + h) * P, "proj", h * P, F, True, True)
+            else:
+                bw = t - N_W - N_Q
+                for i in range(2):
+                    banks[(t, i)] = psum_a.tile([P, 2, KC], F32, name="acc", tag="acc")
+                    for x in range(2):
+                        h = 2 * i + x
+                        mx(banks[(t, i)][:, x, :], N_W + bw // 2, (H * (bw % 2) + h) * P, t, h * KC, KC, True, True)
+
+        def finish(t):
+            if t < N_W:
+                if t % 2 == 0:
+                    return
+                hcols = slice((t // 2) * P, (t // 2 + 1) * P)
+                pg = grp.tile([P, F, 4], BF16, name="pg", tag="pg", align_bytes=64)
+                nc.vector.tensor_copy(out=pg[:], in_=banks[t][:].rearrange("p t f -> p f t"))
+                nc.vector.quantize_mx(
+                    out=pcodes[:, hcols].bitcast(FP8X4), scales=pscales[:, hcols], in_=pg[:].rearrange("p f t -> p (f t)")
+                )
+            elif t < N_W + N_Q:
+                j = t - N_W
+                stage = stages[j % 2]
+                for s in range(2):
+                    nc.scalar.copy(out=stage[:, H * s : H * (s + 1), 0:F], in_=banks[(t, s)][:])
+                first = SCRATCH + j * PAIR
+                nc.scalar.dma_start(
+                    out=outflat[first : first + PAIR].rearrange("(u y) -> u y", y=PAIR_ROW),
+                    in_=stage[:].rearrange("p k x -> p (k x)"),
+                )
+            else:
+                bw = t - N_W - N_Q
+                total = outp.tile([P, H, KC], F32, name="total", tag="total")
+                for i in range(2):
+                    nc.vector.tensor_tensor(
+                        out=total[:, 2 * i : 2 * i + 2, :],
+                        in0=banks[(t, i)][:],
+                        in1=shifted[:, bw * H + 2 * i : bw * H + 2 * i + 2, :],
+                        op=mybir.AluOpType.add,
+                    )
+                for a in range(GROUPS):
+                    nc.sync.dma_start(
+                        out=out[bw // W, :, bw % W, a * QUAD : (a + 1) * QUAD, :].rearrange("h r c -> r h c"),
+                        in_=total[a:P:GROUPS, :, :],
+                    )
+
+        def read_back(t):
+            j = t - N_W
+            for a in range(GROUPS):
+                first = SCRATCH + j * PAIR + a * PAIR_ROW
+                rows = outflat[first : first + QUAD * (GROUPS * PAIR_ROW - 1)].rearrange(
+                    "(r y) -> r y", y=GROUPS * PAIR_ROW - 1
+                )
+                nc.sync.dma_start(
+                    out=shifted[a:P:GROUPS, 2 * H * j : 2 * H * (j + 1), a * QUAD : a * QUAD + WIN],
+                    in_=rows[:, 0:PAIR_ROW].rearrange("r (k x) -> r k x", x=PITCH)[:, :, 0:WIN],
+                )
+
+        gs = const.tile([P, 4, P, 4], BF16, align_bytes=64)
+        for i in range(2):
+            transpose_rows(sraw[:].bitcast(F32), 4 * i, ident, gs[:].bitcast(F32)[:, 2 * i : 2 * i + 2, :, :], i == 1)
+        nc.vector.quantize_mx(
+            out=scodes[:].bitcast(FP8X4), scales=sscales[:], in_=gs[:].rearrange("p c r t -> p (c r t)")
+        )
+        codes["sin"], scales["sin"] = scodes[:], sscales[:]
+        codes["proj"], scales["proj"] = pcodes[:], pscales[:]
+
+        for t in range(N_TILES + 2):
+            if 1 <= t <= N_TILES:
+                quantise(t - 1)
+            if t < N_W:
+                nc.vector.memset(shifted[:, H * t : H * (t + 1), :], 0.0)
+            if t >= 2:
+                finish(t - 2)
+            if N_W <= t - 4 < N_W + N_Q:
+                read_back(t - 4)
+            if t < N_TILES:
+                transpose(t)
+            if t + DEPTH < N_TILES:
+                load(t + DEPTH)
+            if 1 <= t <= N_TILES:
+                multiply(t - 1)

@@ -5,6 +5,7 @@ from concourse.masks import make_identity
 
 F32 = mybir.dt.float32
 BF16 = mybir.dt.bfloat16
+I32 = mybir.dt.int32
 U32 = mybir.dt.uint32
 U8 = mybir.dt.uint8
 FP8X4 = mybir.dt.float8_e4m3fn_x4
@@ -14,15 +15,20 @@ B, W, U, H, D, KC, F = 2, 4, 128, 4, 512, 256, 128
 CH = H * D
 PITCH = 160
 WIN = PITCH - 1
+NK = 2 * H
 QUAD = 32
 GROUPS = U // QUAD
-PAIR_ROW = 2 * H * PITCH
+PAIR_ROW = NK * PITCH
 PAIR = U * PAIR_ROW
-SCRATCH = B * H * W * U * KC - 4 * PAIR - 4096
+N_PAIRS = B * W // 2
+REGION = PAIR + GROUPS * PAIR_ROW
+SCRATCH = B * H * W * U * KC - N_PAIRS * REGION
 
 N_W, N_Q, N_K = 8, 4, 8
 N_TILES = N_W + N_Q + N_K
-DEPTH = 4
+DEPTH = 5
+SPLIT_SLOT = {t: (1,) for t in range(12)}
+ON_VECTOR = 2
 
 FLOPS = 2 * F * CH * CH + B * W * H * 2 * U * D * (KC + F)
 
@@ -32,15 +38,16 @@ def tile_gemma3naudiorelativepositionembedding_pa_kernel(tc, queries, keys, sin_
     with ExitStack() as ctx:
         const = ctx.enter_context(tc.tile_pool(name="const", bufs=1))
         rawp = ctx.enter_context(tc.tile_pool(name="rawp", bufs=DEPTH))
+        evenp = ctx.enter_context(tc.tile_pool(name="evenp", bufs=3))
         grp = ctx.enter_context(tc.tile_pool(name="grp", bufs=3))
-        cod = ctx.enter_context(tc.tile_pool(name="cod", bufs=3))
-        outp = ctx.enter_context(tc.tile_pool(name="outp", bufs=3))
+        cod = ctx.enter_context(tc.tile_pool(name="cod", bufs=5))
+        outp = ctx.enter_context(tc.tile_pool(name="outp", bufs=4))
         psum_t = ctx.enter_context(tc.psum_pool(name="psumt", bufs=4))
         psum_a = ctx.enter_context(tc.psum_pool(name="psuma", bufs=4))
         ctx.enter_context(tc.manual_schedule())
 
         outflat = out.rearrange("b h w u c -> (b h w u c)")
-        raw, grouped, codes, scales, banks = {}, {}, {}, {}, {}
+        raw, halves, grouped, codes, scales, banks = {}, {}, {}, {}, {}, {}
 
         def load(t):
             raw[t] = rawp.tile([P, 2, CH], BF16, name="raw", tag="raw")
@@ -53,10 +60,29 @@ def tile_gemma3naudiorelativepositionembedding_pa_kernel(tc, queries, keys, sin_
             else:
                 bw = t - N_W - N_Q
                 src = keys[bw // W, bw % W].rearrange("(p e) h d -> p e (h d)", e=2)
-            nc.sync.dma_start(out=raw[t][:], in_=src)
+            if t == 0:
+                for e in range(2):
+                    nc.sync.dma_start(out=raw[t][:, e, :], in_=src[:, e, :])
+            else:
+                nc.sync.dma_start(out=raw[t][:], in_=src)
+            for e in range(2):
+                halves[(t, e)] = every_second(raw[t][:, e, :])
+
+        def every_second(row):
+            words = row.bitcast(F32)
+            return [words[:, u : CH // 2 : 2] for u in range(2)]
+
+        def split(t):
+            for e in SPLIT_SLOT.get(t, ()):
+                even = evenp.tile([P, 2, CH // 4], F32, name="even", tag="even")
+                words = raw[t][:, e, :].bitcast(F32).rearrange("p (w u) -> p w u", u=2)
+                nc.vector.tensor_copy(out=even[:].rearrange("p u w -> p w u"), in_=words)
+                halves[(t, e)] = [even[:, u, :] for u in range(2)]
 
         sraw = const.tile([P, CH], BF16)
-        nc.sync.dma_start(out=sraw[:], in_=sin_emb)
+        for i in range(2):
+            half = slice(i * (CH // 2), (i + 1) * (CH // 2))
+            nc.sync.dma_start(out=sraw[:, half], in_=sin_emb[:, half])
         for t in range(DEPTH):
             load(t)
 
@@ -66,11 +92,14 @@ def tile_gemma3naudiorelativepositionembedding_pa_kernel(tc, queries, keys, sin_
         nc.vector.tensor_copy(
             out=perm[:].rearrange("p (r a) -> p a r", a=GROUPS), in_=ident[:].rearrange("p (a r) -> p a r", a=GROUPS)
         )
-        shifted = const.tile([P, B * W * H, KC], F32)
+        shifted = []
+        for j in range(N_PAIRS):
+            pair = const.tile([P, KC, NK], F32, name="shifted%d" % j, align_bytes=64)
+            shifted.append(pair)
         stages = []
         for n in range(2):
-            stage = const.tile([P, 2 * H, PITCH], F32, name="stage%d" % n)
-            nc.vector.memset(stage[:, :, F:PITCH], 0.0)
+            stage = const.tile([P, PITCH, NK], F32, name="stage%d" % n, align_bytes=64)
+            nc.gpsimd.memset(stage[:, F:PITCH, :], 0.0)
             stages.append(stage)
 
         qcodes = const.tile([P, N_Q, 2 * H * U], U32, align_bytes=64)
@@ -90,18 +119,15 @@ def tile_gemma3naudiorelativepositionembedding_pa_kernel(tc, queries, keys, sin_
             bank = psum_t.tile([P, 2, 2, P], F32, name="xt", tag="xt")
             for x in range(2):
                 for u in range(2):
-                    w0 = (first + 2 * x) * P
-                    nc.tensor.transpose(bank[:, x, u, :], words[:, w0 + u : w0 + 2 * P : 2], eye[:])
+                    c = first // 2 + x
+                    nc.tensor.transpose(bank[:, x, u, :], words[u][:, c * P : (c + 1) * P], eye[:])
             copy_out(on_vector, dst, bank[:].rearrange("p x u r -> p x r u"))
 
         def transpose_keys(t, h, dst, on_vector):
             bank = psum_t.tile([P, 2, 2, P], F32, name="xt", tag="xt")
             for e in range(2):
                 for u in range(2):
-                    w0 = 2 * h * P
-                    nc.tensor.transpose(
-                        bank[:, e, u, :], raw[t][:, e, :].bitcast(F32)[:, w0 + u : w0 + 2 * P : 2], ident[:]
-                    )
+                    nc.tensor.transpose(bank[:, e, u, :], halves[(t, e)][u][:, h * P : (h + 1) * P], ident[:])
             copy_out(on_vector, dst, bank[:].rearrange("p e u r -> p r e u"))
 
         def transpose(t):
@@ -111,8 +137,8 @@ def tile_gemma3naudiorelativepositionembedding_pa_kernel(tc, queries, keys, sin_
                 if t < N_W + N_Q:
                     dst = words[:, n, :, :].rearrange("p (x r) u -> p x r u", x=2)
                     eye = ident if t < N_W else perm
-                    on_vector = t >= N_W and n >= 2
-                    transpose_rows(raw[t][:, n // 2, :].bitcast(F32), 4 * (n % 2), eye, dst, on_vector)
+                    on_vector = t >= N_W and n >= ON_VECTOR
+                    transpose_rows(halves[(t, n // 2)], 4 * (n % 2), eye, dst, on_vector)
                 else:
                     dst = words[:, n, :, :].rearrange("p (r e) u -> p r e u", e=2)
                     transpose_keys(t, n, dst, False)
@@ -177,20 +203,23 @@ def tile_gemma3naudiorelativepositionembedding_pa_kernel(tc, queries, keys, sin_
                 j = t - N_W
                 stage = stages[j % 2]
                 for s in range(2):
-                    nc.scalar.copy(out=stage[:, H * s : H * (s + 1), 0:F], in_=banks[(t, s)][:])
-                first = SCRATCH + j * PAIR
+                    nc.scalar.copy(
+                        out=stage[:, 0:F, H * s : H * (s + 1)], in_=banks[(t, s)][:].rearrange("p h f -> p f h")
+                    )
+                first = SCRATCH + j * REGION
                 nc.scalar.dma_start(
                     out=outflat[first : first + PAIR].rearrange("(u y) -> u y", y=PAIR_ROW),
-                    in_=stage[:].rearrange("p k x -> p (k x)"),
+                    in_=stage[:].rearrange("p x k -> p (x k)"),
                 )
             else:
                 bw = t - N_W - N_Q
                 total = outp.tile([P, H, KC], F32, name="total", tag="total")
                 for i in range(2):
+                    k = H * (bw % 2) + 2 * i
                     nc.vector.tensor_tensor(
-                        out=total[:, 2 * i : 2 * i + 2, :],
-                        in0=banks[(t, i)][:],
-                        in1=shifted[:, bw * H + 2 * i : bw * H + 2 * i + 2, :],
+                        out=total[:, 2 * i : 2 * i + 2, :].rearrange("p h c -> p c h"),
+                        in0=banks[(t, i)][:].rearrange("p h c -> p c h"),
+                        in1=shifted[bw // 2][:, :, k : k + 2],
                         op=mybir.AluOpType.add,
                     )
                 for a in range(GROUPS):
@@ -202,36 +231,48 @@ def tile_gemma3naudiorelativepositionembedding_pa_kernel(tc, queries, keys, sin_
         def read_back(t):
             j = t - N_W
             for a in range(GROUPS):
-                first = SCRATCH + j * PAIR + a * PAIR_ROW
-                rows = outflat[first : first + QUAD * (GROUPS * PAIR_ROW - 1)].rearrange(
-                    "(r y) -> r y", y=GROUPS * PAIR_ROW - 1
-                )
+                first = SCRATCH + j * REGION + a * PAIR_ROW
+                step = GROUPS * PAIR_ROW - NK
+                rows = outflat[first : first + QUAD * step].rearrange("(r y) -> r y", y=step)
                 nc.sync.dma_start(
-                    out=shifted[a:P:GROUPS, 2 * H * j : 2 * H * (j + 1), a * QUAD : a * QUAD + WIN],
-                    in_=rows[:, 0:PAIR_ROW].rearrange("r (k x) -> r k x", x=PITCH)[:, :, 0:WIN],
+                    out=shifted[j][a:P:GROUPS, a * QUAD : a * QUAD + WIN, :].rearrange("p x k -> p (x k)"),
+                    in_=rows[:, 0 : WIN * NK],
                 )
+
+        def clear(j, high):
+            first, last = (WIN, KC) if high else (0, U - QUAD)
+            nc.vector.memset(shifted[j][:, first:last, :].rearrange("p x k -> p (x k)").bitcast(I32), 0)
+
+        for j in range(2):
+            for high in range(2):
+                clear(j, high)
 
         gs = const.tile([P, 4, P, 4], BF16, align_bytes=64)
         for i in range(2):
-            transpose_rows(sraw[:].bitcast(F32), 4 * i, ident, gs[:].bitcast(F32)[:, 2 * i : 2 * i + 2, :, :], i == 1)
+            transpose_rows(every_second(sraw[:]), 4 * i, ident, gs[:].bitcast(F32)[:, 2 * i : 2 * i + 2, :, :], i == 1)
         nc.vector.quantize_mx(
             out=scodes[:].bitcast(FP8X4), scales=sscales[:], in_=gs[:].rearrange("p c r t -> p (c r t)")
         )
         codes["sin"], scales["sin"] = scodes[:], sscales[:]
         codes["proj"], scales["proj"] = pcodes[:], pscales[:]
 
+        split(0)
+        k0 = N_W + N_Q
+        multiplies = {t + 1: [t] for t in range(k0)}
+        multiplies.update({t + 1: [t] for t in range(k0, k0 + 8)})
         for t in range(N_TILES + 2):
             if 1 <= t <= N_TILES:
                 quantise(t - 1)
-            if t < N_W:
-                nc.vector.memset(shifted[:, H * t : H * (t + 1), :], 0.0)
-            if t >= 2:
-                finish(t - 2)
-            if N_W <= t - 4 < N_W + N_Q:
-                read_back(t - 4)
+            split(t + 1)
+            if 1 <= t <= 4:
+                clear(2 + (t - 1) // 2, t % 2)
+            for m in multiplies.get(t - 1, []):
+                finish(m)
             if t < N_TILES:
                 transpose(t)
             if t + DEPTH < N_TILES:
                 load(t + DEPTH)
-            if 1 <= t <= N_TILES:
-                multiply(t - 1)
+            if N_W <= t - 3 < N_W + N_Q:
+                read_back(t - 3)
+            for m in multiplies.get(t, []):
+                multiply(m)

@@ -40,7 +40,7 @@ def tile_gemma3naudiorelativepositionembedding_pa_kernel(tc, queries, keys, sin_
         rawp = ctx.enter_context(tc.tile_pool(name="rawp", bufs=DEPTH))
         evenp = ctx.enter_context(tc.tile_pool(name="evenp", bufs=3))
         grp = ctx.enter_context(tc.tile_pool(name="grp", bufs=3))
-        cod = ctx.enter_context(tc.tile_pool(name="cod", bufs=5))
+        cod = ctx.enter_context(tc.tile_pool(name="cod", bufs=3))
         outp = ctx.enter_context(tc.tile_pool(name="outp", bufs=4))
         psum_t = ctx.enter_context(tc.psum_pool(name="psumt", bufs=4))
         psum_a = ctx.enter_context(tc.psum_pool(name="psuma", bufs=4))
@@ -97,7 +97,7 @@ def tile_gemma3naudiorelativepositionembedding_pa_kernel(tc, queries, keys, sin_
             pair = const.tile([P, KC, NK], F32, name="shifted%d" % j, align_bytes=64)
             shifted.append(pair)
         stages = []
-        for n in range(2):
+        for n in range(N_PAIRS):
             stage = const.tile([P, PITCH, NK], F32, name="stage%d" % n, align_bytes=64)
             nc.gpsimd.memset(stage[:, F:PITCH, :], 0.0)
             stages.append(stage)
@@ -130,10 +130,11 @@ def tile_gemma3naudiorelativepositionembedding_pa_kernel(tc, queries, keys, sin_
                     nc.tensor.transpose(bank[:, e, u, :], halves[(t, e)][u][:, h * P : (h + 1) * P], ident[:])
             copy_out(on_vector, dst, bank[:].rearrange("p e u r -> p r e u"))
 
-        def transpose(t):
-            grouped[t] = grp.tile([P, 4, 2 * P, 4], BF16, name="grouped", tag="grouped", align_bytes=64)
+        def transpose(t, part):
+            if part == 0:
+                grouped[t] = grp.tile([P, 4, 2 * P, 4], BF16, name="grouped", tag="grouped", align_bytes=64)
             words = grouped[t][:].bitcast(F32)
-            for n in range(4):
+            for n in (2 * part, 2 * part + 1):
                 if t < N_W + N_Q:
                     dst = words[:, n, :, :].rearrange("p (x r) u -> p x r u", x=2)
                     eye = ident if t < N_W else perm
@@ -201,7 +202,7 @@ def tile_gemma3naudiorelativepositionembedding_pa_kernel(tc, queries, keys, sin_
                 )
             elif t < N_W + N_Q:
                 j = t - N_W
-                stage = stages[j % 2]
+                stage = stages[j]
                 for s in range(2):
                     nc.scalar.copy(
                         out=stage[:, 0:F, H * s : H * (s + 1)], in_=banks[(t, s)][:].rearrange("p h f -> p f h")
@@ -257,22 +258,26 @@ def tile_gemma3naudiorelativepositionembedding_pa_kernel(tc, queries, keys, sin_
         codes["proj"], scales["proj"] = pcodes[:], pscales[:]
 
         split(0)
-        k0 = N_W + N_Q
-        multiplies = {t + 1: [t] for t in range(k0)}
-        multiplies.update({t + 1: [t] for t in range(k0, k0 + 8)})
+        last = N_TILES - 1
         for t in range(N_TILES + 2):
+            if t == N_TILES:
+                finish(last - 1)
             if 1 <= t <= N_TILES:
                 quantise(t - 1)
             split(t + 1)
             if 1 <= t <= 4:
                 clear(2 + (t - 1) // 2, t % 2)
-            for m in multiplies.get(t - 1, []):
-                finish(m)
+            if t >= 2 and t != N_TILES:
+                finish(t - 2)
             if t < N_TILES:
-                transpose(t)
+                transpose(t, 0)
+            if t == last:
+                multiply(last - 1)
+            if t < N_TILES:
+                transpose(t, 1)
             if t + DEPTH < N_TILES:
                 load(t + DEPTH)
             if N_W <= t - 3 < N_W + N_Q:
                 read_back(t - 3)
-            for m in multiplies.get(t, []):
-                multiply(m)
+            if 1 <= t <= N_TILES and t != last:
+                multiply(t - 1)

@@ -13,22 +13,23 @@ FP8X4 = mybir.dt.float8_e4m3fn_x4
 P = 128
 B, W, U, H, D, KC, F = 2, 4, 128, 4, 512, 256, 128
 CH = H * D
-PITCH = 160
-WIN = PITCH - 1
-NK = 2 * H
-QUAD = 32
-GROUPS = U // QUAD
-PAIR_ROW = NK * PITCH
-PAIR = U * PAIR_ROW
 N_PAIRS = B * W // 2
-REGION = PAIR + GROUPS * PAIR_ROW
+NK = 2 * H
+
+GROUP = 32
+GROUPS = U // GROUP
+PITCH = F + GROUP
+WINDOW = F + GROUP - 1
+ROW = PITCH * NK
+PAIR = U * ROW
+REGION = PAIR + GROUPS * ROW
 SCRATCH = B * H * W * U * KC - N_PAIRS * REGION
 
-N_W, N_Q, N_K = 8, 4, 8
-N_TILES = N_W + N_Q + N_K
-DEPTH = 5
-SPLIT_SLOT = {t: (1,) for t in range(12)}
-ON_VECTOR = 2
+FIRST_Q, FIRST_K, N_TILES = 8, 12, 20
+DEPTH = 6
+IN_HALVES = 3
+SPLIT = range(3, N_TILES - 2)
+BOTH_COPY = range(FIRST_K, FIRST_K + 2)
 
 FLOPS = 2 * F * CH * CH + B * W * H * 2 * U * D * (KC + F)
 
@@ -41,26 +42,30 @@ def tile_gemma3naudiorelativepositionembedding_pa_kernel(tc, queries, keys, sin_
         evenp = ctx.enter_context(tc.tile_pool(name="evenp", bufs=3))
         grp = ctx.enter_context(tc.tile_pool(name="grp", bufs=3))
         cod = ctx.enter_context(tc.tile_pool(name="cod", bufs=3))
-        outp = ctx.enter_context(tc.tile_pool(name="outp", bufs=4))
+        outp = ctx.enter_context(tc.tile_pool(name="outp", bufs=6))
         psum_t = ctx.enter_context(tc.psum_pool(name="psumt", bufs=4))
         psum_a = ctx.enter_context(tc.psum_pool(name="psuma", bufs=4))
         ctx.enter_context(tc.manual_schedule())
 
         outflat = out.rearrange("b h w u c -> (b h w u c)")
-        raw, halves, grouped, codes, scales, banks = {}, {}, {}, {}, {}, {}
+        raw, halves, grouped, codes, scales, banks, projs = {}, {}, {}, {}, {}, {}, {}
+
+        def every_second(row):
+            words = row.bitcast(F32)
+            return [words[:, u : CH // 2 : 2] for u in range(2)]
 
         def load(t):
             raw[t] = rawp.tile([P, 2, CH], BF16, name="raw", tag="raw")
-            if t < N_W:
-                four = pos_w[D * (t // 2) : D * (t // 2 + 1), :].rearrange("(p e) c -> p e c", e=4)
-                src = four[:, 2 * (t % 2) : 2 * (t % 2) + 2, :]
-            elif t < N_W + N_Q:
-                j = t - N_W
+            if t < FIRST_Q:
+                head = pos_w[D * (t // 2) : D * (t // 2 + 1), :].rearrange("(p e) c -> p e c", e=4)
+                src = head[:, 2 * (t % 2) : 2 * (t % 2) + 2, :]
+            elif t < FIRST_K:
+                j = t - FIRST_Q
                 src = queries[j // 2, 2 * (j % 2) : 2 * (j % 2) + 2].rearrange("s u h d -> u s (h d)")
             else:
-                bw = t - N_W - N_Q
-                src = keys[bw // W, bw % W].rearrange("(p e) h d -> p e (h d)", e=2)
-            if t == 0:
+                item = t - FIRST_K
+                src = keys[item // W, item % W].rearrange("(p e) h d -> p e (h d)", e=2)
+            if t < IN_HALVES:
                 for e in range(2):
                     nc.sync.dma_start(out=raw[t][:, e, :], in_=src[:, e, :])
             else:
@@ -68,16 +73,12 @@ def tile_gemma3naudiorelativepositionembedding_pa_kernel(tc, queries, keys, sin_
             for e in range(2):
                 halves[(t, e)] = every_second(raw[t][:, e, :])
 
-        def every_second(row):
-            words = row.bitcast(F32)
-            return [words[:, u : CH // 2 : 2] for u in range(2)]
-
         def split(t):
-            for e in SPLIT_SLOT.get(t, ()):
+            if t in SPLIT:
                 even = evenp.tile([P, 2, CH // 4], F32, name="even", tag="even")
-                words = raw[t][:, e, :].bitcast(F32).rearrange("p (w u) -> p w u", u=2)
+                words = raw[t][:, 1, :].bitcast(F32).rearrange("p (w u) -> p w u", u=2)
                 nc.vector.tensor_copy(out=even[:].rearrange("p u w -> p w u"), in_=words)
-                halves[(t, e)] = [even[:, u, :] for u in range(2)]
+                halves[(t, 1)] = [even[:, u, :] for u in range(2)]
 
         sraw = const.tile([P, CH], BF16)
         for i in range(2):
@@ -92,18 +93,17 @@ def tile_gemma3naudiorelativepositionembedding_pa_kernel(tc, queries, keys, sin_
         nc.vector.tensor_copy(
             out=perm[:].rearrange("p (r a) -> p a r", a=GROUPS), in_=ident[:].rearrange("p (a r) -> p a r", a=GROUPS)
         )
-        shifted = []
+        shifted, stages = [], []
         for j in range(N_PAIRS):
-            pair = const.tile([P, KC, NK], F32, name="shifted%d" % j, align_bytes=64)
-            shifted.append(pair)
-        stages = []
-        for n in range(N_PAIRS):
-            stage = const.tile([P, PITCH, NK], F32, name="stage%d" % n, align_bytes=64)
+            moved = const.tile([P, KC, NK], F32, name="shifted%d" % j, align_bytes=64)
+            shifted.append(moved)
+        for j in range(N_PAIRS):
+            stage = const.tile([P, PITCH, NK], F32, name="stage%d" % j, align_bytes=64)
             nc.gpsimd.memset(stage[:, F:PITCH, :], 0.0)
             stages.append(stage)
 
-        qcodes = const.tile([P, N_Q, 2 * H * U], U32, align_bytes=64)
-        qscales = const.tile([P, N_Q, 2 * H * U], U8, align_bytes=64)
+        qcodes = const.tile([P, N_PAIRS, 2 * H * U], U32, align_bytes=64)
+        qscales = const.tile([P, N_PAIRS, 2 * H * U], U8, align_bytes=64)
         scodes = const.tile([P, 4 * F], U32, align_bytes=64)
         sscales = const.tile([P, 4 * F], U8, align_bytes=64)
         pcodes = const.tile([P, H * F], U32, align_bytes=64)
@@ -115,134 +115,134 @@ def tile_gemma3naudiorelativepositionembedding_pa_kernel(tc, queries, keys, sin_
             else:
                 nc.scalar.copy(out=dst, in_=src)
 
-        def transpose_rows(words, first, eye, dst, on_vector):
+        def transpose_passes(words, first, eye, dst, on_vector):
             bank = psum_t.tile([P, 2, 2, P], F32, name="xt", tag="xt")
             for x in range(2):
                 for u in range(2):
-                    c = first // 2 + x
+                    c = first + x
                     nc.tensor.transpose(bank[:, x, u, :], words[u][:, c * P : (c + 1) * P], eye[:])
-            copy_out(on_vector, dst, bank[:].rearrange("p x u r -> p x r u"))
+            copy_out(on_vector, dst.rearrange("p (x r) u -> p x r u", x=2), bank[:].rearrange("p x u r -> p x r u"))
 
         def transpose_keys(t, h, dst, on_vector):
             bank = psum_t.tile([P, 2, 2, P], F32, name="xt", tag="xt")
             for e in range(2):
                 for u in range(2):
                     nc.tensor.transpose(bank[:, e, u, :], halves[(t, e)][u][:, h * P : (h + 1) * P], ident[:])
-            copy_out(on_vector, dst, bank[:].rearrange("p e u r -> p r e u"))
+            copy_out(on_vector, dst.rearrange("p (r e) u -> p r e u", e=2), bank[:].rearrange("p e u r -> p r e u"))
 
         def transpose(t, part):
             if part == 0:
                 grouped[t] = grp.tile([P, 4, 2 * P, 4], BF16, name="grouped", tag="grouped", align_bytes=64)
             words = grouped[t][:].bitcast(F32)
             for n in (2 * part, 2 * part + 1):
-                if t < N_W + N_Q:
-                    dst = words[:, n, :, :].rearrange("p (x r) u -> p x r u", x=2)
-                    eye = ident if t < N_W else perm
-                    on_vector = t >= N_W and n >= ON_VECTOR
-                    transpose_rows(halves[(t, n // 2)], 4 * (n % 2), eye, dst, on_vector)
+                if t < FIRST_Q:
+                    transpose_passes(halves[(t, n // 2)], 2 * (n % 2), ident, words[:, n, :, :], False)
+                elif t < FIRST_K:
+                    transpose_passes(halves[(t, n // 2)], 2 * (n % 2), perm, words[:, n, :, :], part == 1)
                 else:
-                    dst = words[:, n, :, :].rearrange("p (r e) u -> p r e u", e=2)
-                    transpose_keys(t, n, dst, False)
+                    transpose_keys(t, n, words[:, n, :, :], t in BOTH_COPY and n == 3)
 
-        def quantise(t):
-            if N_W <= t < N_W + N_Q:
-                codes[t], scales[t] = qcodes[:, t - N_W, :], qscales[:, t - N_W, :]
-            else:
-                ctile = cod.tile([P, 8 * P], U32, name="ctile", tag="ctile", align_bytes=64)
-                stile = cod.tile([P, 8 * P], U8, name="stile", tag="stile", align_bytes=64)
-                codes[t], scales[t] = ctile[:], stile[:]
-            for n in range(2):
-                cols = slice(4 * P * n, 4 * P * (n + 1))
-                nc.vector.quantize_mx(
-                    out=codes[t][:, cols].bitcast(FP8X4),
-                    scales=scales[t][:, cols],
-                    in_=grouped[t][:, 2 * n : 2 * n + 2].rearrange("p n c t -> p (n c t)"),
-                )
+        def quantise(t, part):
+            if part == 0:
+                if FIRST_Q <= t < FIRST_K:
+                    codes[t], scales[t] = qcodes[:, t - FIRST_Q, :], qscales[:, t - FIRST_Q, :]
+                else:
+                    ctile = cod.tile([P, 8 * P], U32, name="ctile", tag="ctile", align_bytes=64)
+                    stile = cod.tile([P, 8 * P], U8, name="stile", tag="stile", align_bytes=64)
+                    codes[t], scales[t] = ctile[:], stile[:]
+            cols = slice(4 * P * part, 4 * P * (part + 1))
+            nc.vector.quantize_mx(
+                out=codes[t][:, cols].bitcast(FP8X4),
+                scales=scales[t][:, cols],
+                in_=grouped[t][:, 2 * part : 2 * part + 2].rearrange("p n c k -> p (n c k)"),
+            )
 
-        def mx(dst, t_l, l0, t_r, r0, n, start, stop):
+        def mx(dst, left, l0, right, r0, n, start, stop):
             nc.tensor.matmul_mx(
                 out=dst,
-                lhsT=codes[t_l][:, l0 : l0 + P].bitcast(FP8X4),
-                lhsT_scale=scales[t_l][:, l0 : l0 + P],
-                rhs=codes[t_r][:, r0 : r0 + n].bitcast(FP8X4),
-                rhs_scale=scales[t_r][:, r0 : r0 + n],
+                lhsT=codes[left][:, l0 : l0 + P].bitcast(FP8X4),
+                lhsT_scale=scales[left][:, l0 : l0 + P],
+                rhs=codes[right][:, r0 : r0 + n].bitcast(FP8X4),
+                rhs_scale=scales[right][:, r0 : r0 + n],
                 start=start,
                 stop=stop,
             )
 
         def multiply(t):
-            if t < N_W:
+            if t < FIRST_Q:
                 if t % 2 == 0:
-                    banks[t + 1] = psum_a.tile([P, 4, F], F32, name="acc", tag="acc")
+                    banks[t // 2] = psum_a.tile([P, 4, F], F32, name="acc", tag="acc")
                 for e in range(2):
                     for c in range(4):
-                        mx(banks[t | 1][:, 2 * (t % 2) + e, :], t, (4 * e + c) * P, "sin", c * P, F, c == 0, c == 3)
-            elif t < N_W + N_Q:
+                        mx(banks[t // 2][:, 2 * (t % 2) + e, :], t, (4 * e + c) * P, "sin", c * P, F, c == 0, c == 3)
+            elif t < FIRST_K:
                 for s in range(2):
                     banks[(t, s)] = psum_a.tile([P, H, F], F32, name="acc", tag="acc")
                     for h in range(H):
                         mx(banks[(t, s)][:, h, :], t, (H * s + h) * P, "proj", h * P, F, True, True)
             else:
-                bw = t - N_W - N_Q
+                item = t - FIRST_K
                 for i in range(2):
                     banks[(t, i)] = psum_a.tile([P, 2, KC], F32, name="acc", tag="acc")
                     for x in range(2):
                         h = 2 * i + x
-                        mx(banks[(t, i)][:, x, :], N_W + bw // 2, (H * (bw % 2) + h) * P, t, h * KC, KC, True, True)
+                        q0 = (H * (item % 2) + h) * P
+                        mx(banks[(t, i)][:, x, :], FIRST_Q + item // 2, q0, t, h * KC, KC, True, True)
 
-        def finish(t):
-            if t < N_W:
-                if t % 2 == 0:
-                    return
-                hcols = slice((t // 2) * P, (t // 2 + 1) * P)
-                pg = grp.tile([P, F, 4], BF16, name="pg", tag="pg", align_bytes=64)
-                nc.vector.tensor_copy(out=pg[:], in_=banks[t][:].rearrange("p t f -> p f t"))
-                nc.vector.quantize_mx(
-                    out=pcodes[:, hcols].bitcast(FP8X4), scales=pscales[:, hcols], in_=pg[:].rearrange("p f t -> p (f t)")
+        def round_proj(h):
+            projs[h] = grp.tile([P, F, 4], BF16, name="proj", tag="proj", align_bytes=64)
+            nc.vector.tensor_copy(out=projs[h][:], in_=banks[h][:].rearrange("p k f -> p f k"))
+
+        def quantise_proj(h):
+            cols = slice(h * F, (h + 1) * F)
+            nc.vector.quantize_mx(
+                out=pcodes[:, cols].bitcast(FP8X4), scales=pscales[:, cols], in_=projs[h][:].rearrange("p f k -> p (f k)")
+            )
+
+        def store_bd(t):
+            j = t - FIRST_Q
+            for s in range(2):
+                nc.scalar.copy(
+                    out=stages[j][:, 0:F, H * s : H * (s + 1)], in_=banks[(t, s)][:].rearrange("p h f -> p f h")
                 )
-            elif t < N_W + N_Q:
-                j = t - N_W
-                stage = stages[j]
-                for s in range(2):
-                    nc.scalar.copy(
-                        out=stage[:, 0:F, H * s : H * (s + 1)], in_=banks[(t, s)][:].rearrange("p h f -> p f h")
-                    )
-                first = SCRATCH + j * REGION
-                nc.scalar.dma_start(
-                    out=outflat[first : first + PAIR].rearrange("(u y) -> u y", y=PAIR_ROW),
-                    in_=stage[:].rearrange("p x k -> p (x k)"),
-                )
-            else:
-                bw = t - N_W - N_Q
-                total = outp.tile([P, H, KC], F32, name="total", tag="total")
-                for i in range(2):
-                    k = H * (bw % 2) + 2 * i
-                    nc.vector.tensor_tensor(
-                        out=total[:, 2 * i : 2 * i + 2, :].rearrange("p h c -> p c h"),
-                        in0=banks[(t, i)][:].rearrange("p h c -> p c h"),
-                        in1=shifted[bw // 2][:, :, k : k + 2],
-                        op=mybir.AluOpType.add,
-                    )
-                for a in range(GROUPS):
-                    nc.sync.dma_start(
-                        out=out[bw // W, :, bw % W, a * QUAD : (a + 1) * QUAD, :].rearrange("h r c -> r h c"),
-                        in_=total[a:P:GROUPS, :, :],
-                    )
+            first = SCRATCH + j * REGION
+            nc.scalar.dma_start(
+                out=outflat[first : first + PAIR].rearrange("(u y) -> u y", y=ROW),
+                in_=stages[j][:].rearrange("p x k -> p (x k)"),
+            )
 
         def read_back(t):
-            j = t - N_W
+            j = t - FIRST_Q
+            step = GROUPS * ROW - NK
             for a in range(GROUPS):
-                first = SCRATCH + j * REGION + a * PAIR_ROW
-                step = GROUPS * PAIR_ROW - NK
-                rows = outflat[first : first + QUAD * step].rearrange("(r y) -> r y", y=step)
+                first = SCRATCH + j * REGION + a * ROW
+                rows = outflat[first : first + GROUP * step].rearrange("(r y) -> r y", y=step)
                 nc.sync.dma_start(
-                    out=shifted[j][a:P:GROUPS, a * QUAD : a * QUAD + WIN, :].rearrange("p x k -> p (x k)"),
-                    in_=rows[:, 0 : WIN * NK],
+                    out=shifted[j][a:P:GROUPS, a * GROUP : a * GROUP + WINDOW, :].rearrange("p x k -> p (x k)"),
+                    in_=rows[:, 0 : WINDOW * NK],
                 )
 
         def clear(j, high):
-            first, last = (WIN, KC) if high else (0, U - QUAD)
+            first, last = (WINDOW, KC) if high else (0, U - GROUP)
             nc.vector.memset(shifted[j][:, first:last, :].rearrange("p x k -> p (x k)").bitcast(I32), 0)
+
+        def add_and_store(t):
+            item = t - FIRST_K
+            total = outp.tile([P, H, KC], F32, name="total", tag="total")
+            for i in range(2):
+                k = H * (item % 2) + 2 * i
+                nc.vector.tensor_tensor(
+                    out=total[:, 2 * i : 2 * i + 2, :].rearrange("p h c -> p c h"),
+                    in0=banks[(t, i)][:].rearrange("p h c -> p c h"),
+                    in1=shifted[item // 2][:, :, k : k + 2],
+                    op=mybir.AluOpType.add,
+                )
+            for a in range(GROUPS):
+                rows = slice(a * GROUP, (a + 1) * GROUP)
+                nc.sync.dma_start(
+                    out=out[item // W, :, item % W, rows, :].rearrange("h r c -> r h c"),
+                    in_=total[a:P:GROUPS, :, :],
+                )
 
         for j in range(2):
             for high in range(2):
@@ -250,34 +250,46 @@ def tile_gemma3naudiorelativepositionembedding_pa_kernel(tc, queries, keys, sin_
 
         gs = const.tile([P, 4, P, 4], BF16, align_bytes=64)
         for i in range(2):
-            transpose_rows(every_second(sraw[:]), 4 * i, ident, gs[:].bitcast(F32)[:, 2 * i : 2 * i + 2, :, :], i == 1)
+            dst = gs[:].bitcast(F32)[:, 2 * i : 2 * i + 2, :, :].rearrange("p x r u -> p (x r) u")
+            transpose_passes(every_second(sraw[:]), 2 * i, ident, dst, i == 1)
         nc.vector.quantize_mx(
-            out=scodes[:].bitcast(FP8X4), scales=sscales[:], in_=gs[:].rearrange("p c r t -> p (c r t)")
+            out=scodes[:].bitcast(FP8X4), scales=sscales[:], in_=gs[:].rearrange("p c r k -> p (c r k)")
         )
         codes["sin"], scales["sin"] = scodes[:], sscales[:]
         codes["proj"], scales["proj"] = pcodes[:], pscales[:]
 
-        split(0)
         last = N_TILES - 1
-        for t in range(N_TILES + 2):
-            if t == N_TILES:
-                finish(last - 1)
-            if 1 <= t <= N_TILES:
-                quantise(t - 1)
-            split(t + 1)
+        for t in range(N_TILES + 1):
+            done = t - 2
+            head_done = 0 <= done < FIRST_Q and done % 2 == 1
+            if t >= 1:
+                quantise(t - 1, 0)
+            if head_done:
+                round_proj(done // 2)
+            if t > FIRST_K:
+                split(t + 1)
+            if t >= 1:
+                quantise(t - 1, 1)
+            if head_done:
+                quantise_proj(done // 2)
+            if t <= FIRST_K:
+                split(t + 1)
             if 1 <= t <= 4:
                 clear(2 + (t - 1) // 2, t % 2)
-            if t >= 2 and t != N_TILES:
-                finish(t - 2)
+            if FIRST_Q <= done < FIRST_K:
+                store_bd(done)
+            if FIRST_K <= done < last - 1:
+                add_and_store(done)
             if t < N_TILES:
                 transpose(t, 0)
-            if t == last:
-                multiply(last - 1)
-            if t < N_TILES:
+                if t == last:
+                    multiply(t - 1)
+                    add_and_store(t - 1)
                 transpose(t, 1)
+            if FIRST_Q <= t - 3 < FIRST_K:
+                read_back(t - 3)
             if t + DEPTH < N_TILES:
                 load(t + DEPTH)
-            if N_W <= t - 3 < N_W + N_Q:
-                read_back(t - 3)
-            if 1 <= t <= N_TILES and t != last:
+            if t >= 1 and t != last:
                 multiply(t - 1)
+        add_and_store(last)

from contextlib import ExitStack

import concourse.mybir as mybir
from concourse.masks import make_identity

F32 = mybir.dt.float32
BF16 = mybir.dt.bfloat16
I32 = mybir.dt.int32
U32 = mybir.dt.uint32
U8 = mybir.dt.uint8
FP8X4 = mybir.dt.float8_e4m3fn_x4

P = 128
B, W, U, H, D, KC, F = 2, 4, 128, 4, 512, 256, 128
CH = H * D
N_PAIRS = B * W // 2
NK = 2 * H

GROUP = 32
GROUPS = U // GROUP
PITCH = F + GROUP
WINDOW = F + GROUP - 1
ROW = PITCH * NK
PAIR = U * ROW
REGION = PAIR + GROUPS * ROW
SCRATCH = B * H * W * U * KC - N_PAIRS * REGION

FIRST_Q, FIRST_K, N_TILES = 8, 12, 20
DEPTH = 6
IN_HALVES = 3
SPLIT = range(3, N_TILES - 2)
BOTH_COPY = range(FIRST_K, FIRST_K + 2)

FLOPS = 2 * F * CH * CH + B * W * H * 2 * U * D * (KC + F)


def tile_gemma3naudiorelativepositionembedding_pa_kernel(tc, queries, keys, sin_emb, pos_w, out):
    nc = tc.nc
    with ExitStack() as ctx:
        const = ctx.enter_context(tc.tile_pool(name="const", bufs=1))
        rawp = ctx.enter_context(tc.tile_pool(name="rawp", bufs=DEPTH))
        evenp = ctx.enter_context(tc.tile_pool(name="evenp", bufs=3))
        grp = ctx.enter_context(tc.tile_pool(name="grp", bufs=3))
        cod = ctx.enter_context(tc.tile_pool(name="cod", bufs=3))
        outp = ctx.enter_context(tc.tile_pool(name="outp", bufs=6))
        psum_t = ctx.enter_context(tc.psum_pool(name="psumt", bufs=4))
        psum_a = ctx.enter_context(tc.psum_pool(name="psuma", bufs=4))
        ctx.enter_context(tc.manual_schedule())

        outflat = out.rearrange("b h w u c -> (b h w u c)")
        raw, halves, grouped, codes, scales, banks, projs = {}, {}, {}, {}, {}, {}, {}

        def every_second(row):
            words = row.bitcast(F32)
            return [words[:, u : CH // 2 : 2] for u in range(2)]

        def load(t):
            raw[t] = rawp.tile([P, 2, CH], BF16, name="raw", tag="raw")
            if t < FIRST_Q:
                head = pos_w[D * (t // 2) : D * (t // 2 + 1), :].rearrange("(p e) c -> p e c", e=4)
                src = head[:, 2 * (t % 2) : 2 * (t % 2) + 2, :]
            elif t < FIRST_K:
                j = t - FIRST_Q
                src = queries[j // 2, 2 * (j % 2) : 2 * (j % 2) + 2].rearrange("s u h d -> u s (h d)")
            else:
                item = t - FIRST_K
                src = keys[item // W, item % W].rearrange("(p e) h d -> p e (h d)", e=2)
            if t < IN_HALVES:
                for e in range(2):
                    nc.sync.dma_start(out=raw[t][:, e, :], in_=src[:, e, :])
            else:
                nc.sync.dma_start(out=raw[t][:], in_=src)
            for e in range(2):
                halves[(t, e)] = every_second(raw[t][:, e, :])

        def split(t):
            if t in SPLIT:
                even = evenp.tile([P, 2, CH // 4], F32, name="even", tag="even")
                words = raw[t][:, 1, :].bitcast(F32).rearrange("p (w u) -> p w u", u=2)
                nc.vector.tensor_copy(out=even[:].rearrange("p u w -> p w u"), in_=words)
                halves[(t, 1)] = [even[:, u, :] for u in range(2)]

        sraw = const.tile([P, CH], BF16)
        for i in range(2):
            half = slice(i * (CH // 2), (i + 1) * (CH // 2))
            nc.sync.dma_start(out=sraw[:, half], in_=sin_emb[:, half])
        for t in range(DEPTH):
            load(t)

        ident = const.tile([P, P], F32)
        make_identity(nc, ident[:])
        perm = const.tile([P, P], F32)
        nc.vector.tensor_copy(
            out=perm[:].rearrange("p (r a) -> p a r", a=GROUPS), in_=ident[:].rearrange("p (a r) -> p a r", a=GROUPS)
        )
        shifted, stages = [], []
        for j in range(N_PAIRS):
            moved = const.tile([P, KC, NK], F32, name="shifted%d" % j, align_bytes=64)
            shifted.append(moved)
        for j in range(N_PAIRS):
            stage = const.tile([P, PITCH, NK], F32, name="stage%d" % j, align_bytes=64)
            nc.gpsimd.memset(stage[:, F:PITCH, :], 0.0)
            stages.append(stage)

        qcodes = const.tile([P, N_PAIRS, 2 * H * U], U32, align_bytes=64)
        qscales = const.tile([P, N_PAIRS, 2 * H * U], U8, align_bytes=64)
        scodes = const.tile([P, 4 * F], U32, align_bytes=64)
        sscales = const.tile([P, 4 * F], U8, align_bytes=64)
        pcodes = const.tile([P, H * F], U32, align_bytes=64)
        pscales = const.tile([P, H * F], U8, align_bytes=64)

        def copy_out(on_vector, dst, src):
            if on_vector:
                nc.vector.tensor_copy(out=dst, in_=src)
            else:
                nc.scalar.copy(out=dst, in_=src)

        def transpose_passes(words, first, eye, dst, on_vector):
            bank = psum_t.tile([P, 2, 2, P], F32, name="xt", tag="xt")
            for x in range(2):
                for u in range(2):
                    c = first + x
                    nc.tensor.transpose(bank[:, x, u, :], words[u][:, c * P : (c + 1) * P], eye[:])
            copy_out(on_vector, dst.rearrange("p (x r) u -> p x r u", x=2), bank[:].rearrange("p x u r -> p x r u"))

        def transpose_keys(t, h, dst, on_vector):
            bank = psum_t.tile([P, 2, 2, P], F32, name="xt", tag="xt")
            for e in range(2):
                for u in range(2):
                    nc.tensor.transpose(bank[:, e, u, :], halves[(t, e)][u][:, h * P : (h + 1) * P], ident[:])
            copy_out(on_vector, dst.rearrange("p (r e) u -> p r e u", e=2), bank[:].rearrange("p e u r -> p r e u"))

        def transpose(t, part):
            if part == 0:
                grouped[t] = grp.tile([P, 4, 2 * P, 4], BF16, name="grouped", tag="grouped", align_bytes=64)
            words = grouped[t][:].bitcast(F32)
            for n in (2 * part, 2 * part + 1):
                if t < FIRST_Q:
                    transpose_passes(halves[(t, n // 2)], 2 * (n % 2), ident, words[:, n, :, :], False)
                elif t < FIRST_K:
                    transpose_passes(halves[(t, n // 2)], 2 * (n % 2), perm, words[:, n, :, :], part == 1)
                else:
                    transpose_keys(t, n, words[:, n, :, :], t in BOTH_COPY and n == 3)

        def quantise(t, part):
            if part == 0:
                if FIRST_Q <= t < FIRST_K:
                    codes[t], scales[t] = qcodes[:, t - FIRST_Q, :], qscales[:, t - FIRST_Q, :]
                else:
                    ctile = cod.tile([P, 8 * P], U32, name="ctile", tag="ctile", align_bytes=64)
                    stile = cod.tile([P, 8 * P], U8, name="stile", tag="stile", align_bytes=64)
                    codes[t], scales[t] = ctile[:], stile[:]
            cols = slice(4 * P * part, 4 * P * (part + 1))
            nc.vector.quantize_mx(
                out=codes[t][:, cols].bitcast(FP8X4),
                scales=scales[t][:, cols],
                in_=grouped[t][:, 2 * part : 2 * part + 2].rearrange("p n c k -> p (n c k)"),
            )

        def mx(dst, left, l0, right, r0, n, start, stop):
            nc.tensor.matmul_mx(
                out=dst,
                lhsT=codes[left][:, l0 : l0 + P].bitcast(FP8X4),
                lhsT_scale=scales[left][:, l0 : l0 + P],
                rhs=codes[right][:, r0 : r0 + n].bitcast(FP8X4),
                rhs_scale=scales[right][:, r0 : r0 + n],
                start=start,
                stop=stop,
            )

        def multiply(t):
            if t < FIRST_Q:
                if t % 2 == 0:
                    banks[t // 2] = psum_a.tile([P, 4, F], F32, name="acc", tag="acc")
                for e in range(2):
                    for c in range(4):
                        mx(banks[t // 2][:, 2 * (t % 2) + e, :], t, (4 * e + c) * P, "sin", c * P, F, c == 0, c == 3)
            elif t < FIRST_K:
                for s in range(2):
                    banks[(t, s)] = psum_a.tile([P, H, F], F32, name="acc", tag="acc")
                    for h in range(H):
                        mx(banks[(t, s)][:, h, :], t, (H * s + h) * P, "proj", h * P, F, True, True)
            else:
                item = t - FIRST_K
                for i in range(2):
                    banks[(t, i)] = psum_a.tile([P, 2, KC], F32, name="acc", tag="acc")
                    for x in range(2):
                        h = 2 * i + x
                        q0 = (H * (item % 2) + h) * P
                        mx(banks[(t, i)][:, x, :], FIRST_Q + item // 2, q0, t, h * KC, KC, True, True)

        def round_proj(h):
            projs[h] = grp.tile([P, F, 4], BF16, name="proj", tag="proj", align_bytes=64)
            nc.vector.tensor_copy(out=projs[h][:], in_=banks[h][:].rearrange("p k f -> p f k"))

        def quantise_proj(h):
            cols = slice(h * F, (h + 1) * F)
            nc.vector.quantize_mx(
                out=pcodes[:, cols].bitcast(FP8X4), scales=pscales[:, cols], in_=projs[h][:].rearrange("p f k -> p (f k)")
            )

        def store_bd(t):
            j = t - FIRST_Q
            for s in range(2):
                nc.scalar.copy(
                    out=stages[j][:, 0:F, H * s : H * (s + 1)], in_=banks[(t, s)][:].rearrange("p h f -> p f h")
                )
            first = SCRATCH + j * REGION
            nc.scalar.dma_start(
                out=outflat[first : first + PAIR].rearrange("(u y) -> u y", y=ROW),
                in_=stages[j][:].rearrange("p x k -> p (x k)"),
            )

        def read_back(t):
            j = t - FIRST_Q
            step = GROUPS * ROW - NK
            for a in range(GROUPS):
                first = SCRATCH + j * REGION + a * ROW
                rows = outflat[first : first + GROUP * step].rearrange("(r y) -> r y", y=step)
                nc.sync.dma_start(
                    out=shifted[j][a:P:GROUPS, a * GROUP : a * GROUP + WINDOW, :].rearrange("p x k -> p (x k)"),
                    in_=rows[:, 0 : WINDOW * NK],
                )

        def clear(j, high):
            first, last = (WINDOW, KC) if high else (0, U - GROUP)
            nc.vector.memset(shifted[j][:, first:last, :].rearrange("p x k -> p (x k)").bitcast(I32), 0)

        def add_and_store(t):
            item = t - FIRST_K
            total = outp.tile([P, H, KC], F32, name="total", tag="total")
            for i in range(2):
                k = H * (item % 2) + 2 * i
                nc.vector.tensor_tensor(
                    out=total[:, 2 * i : 2 * i + 2, :].rearrange("p h c -> p c h"),
                    in0=banks[(t, i)][:].rearrange("p h c -> p c h"),
                    in1=shifted[item // 2][:, :, k : k + 2],
                    op=mybir.AluOpType.add,
                )
            for a in range(GROUPS):
                rows = slice(a * GROUP, (a + 1) * GROUP)
                nc.sync.dma_start(
                    out=out[item // W, :, item % W, rows, :].rearrange("h r c -> r h c"),
                    in_=total[a:P:GROUPS, :, :],
                )

        for j in range(2):
            for high in range(2):
                clear(j, high)

        gs = const.tile([P, 4, P, 4], BF16, align_bytes=64)
        for i in range(2):
            dst = gs[:].bitcast(F32)[:, 2 * i : 2 * i + 2, :, :].rearrange("p x r u -> p (x r) u")
            transpose_passes(every_second(sraw[:]), 2 * i, ident, dst, i == 1)
        nc.vector.quantize_mx(
            out=scodes[:].bitcast(FP8X4), scales=sscales[:], in_=gs[:].rearrange("p c r k -> p (c r k)")
        )
        codes["sin"], scales["sin"] = scodes[:], sscales[:]
        codes["proj"], scales["proj"] = pcodes[:], pscales[:]

        last = N_TILES - 1
        for t in range(N_TILES + 1):
            done = t - 2
            head_done = 0 <= done < FIRST_Q and done % 2 == 1
            if t >= 1:
                quantise(t - 1, 0)
            if head_done:
                round_proj(done // 2)
            if t > FIRST_K:
                split(t + 1)
            if t >= 1:
                quantise(t - 1, 1)
            if head_done:
                quantise_proj(done // 2)
            if t <= FIRST_K:
                split(t + 1)
            if 1 <= t <= 4:
                clear(2 + (t - 1) // 2, t % 2)
            if FIRST_Q <= done < FIRST_K:
                store_bd(done)
            if FIRST_K <= done < last - 1:
                add_and_store(done)
            if t < N_TILES:
                transpose(t, 0)
                if t == last:
                    multiply(t - 1)
                    add_and_store(t - 1)
                transpose(t, 1)
            if FIRST_Q <= t - 3 < FIRST_K:
                read_back(t - 3)
            if t + DEPTH < N_TILES:
                load(t + DEPTH)
            if t >= 1 and t != last:
                multiply(t - 1)
        add_and_store(last)
